import numpy as np
import ml_dtypes


def mxq(x, axis, fmt="e4m3"):
    dtype, down = {"e4m3": (ml_dtypes.float8_e4m3fn, 7), "e5m2": (ml_dtypes.float8_e5m2, 14)}[fmt]
    v = np.moveaxis(np.asarray(x, np.float32).astype(ml_dtypes.bfloat16).astype(np.float64), axis, -1)
    blocks = v.reshape(v.shape[:-1] + (-1, 32))
    amax = np.abs(blocks).max(-1, keepdims=True)
    byte = np.maximum(np.where(amax > 0, np.frexp(amax)[1] - 1 + 127, 0) - down, 1)
    scale = np.exp2(byte - 127.0)
    codes = (blocks / scale).astype(np.float32).astype(dtype).astype(np.float64)
    return np.moveaxis((codes * scale).reshape(v.shape), -1, axis)


WIDE = False


def mx_kscale(k):
    if not WIDE:
        return np.ones(k)
    levels = np.array([30, -30])
    if k % 512:
        return np.exp2(np.random.permutation(np.resize(levels, k // 32))).repeat(32)
    a = np.empty((k // 512, 16))
    for p in range(k // 512):
        a[p, :8] = np.random.permutation(np.resize(levels, 8))
        for g in range(8):
            far = levels[np.abs(levels - a[p, g]) >= 10]
            a[p, g + 8] = far[np.random.randint(len(far))]
    return np.exp2(a.ravel()).repeat(32)


BF16 = ml_dtypes.bfloat16


def bf(x):
    return np.asarray(x, np.float32).astype(BF16)


def f64(x):
    return np.asarray(x).astype(np.float64)


B, S, DIM, H, D = 2, 256, 2048, 16, 128
E = H * D
ROPE_THETA = 10000.0


def rope(t):
    inv_freq = 1.0 / ROPE_THETA ** (np.arange(0, D, 2) / D)
    ang = np.arange(S)[:, None] * inv_freq[None, :]
    cos = np.concatenate([np.cos(ang), np.cos(ang)], axis=-1)[None, :, None, :]
    sin = np.concatenate([np.sin(ang), np.sin(ang)], axis=-1)[None, :, None, :]
    t1, t2 = np.split(t, 2, axis=-1)
    rot = np.concatenate([-t2, t1], axis=-1)
    return t * cos + rot * sin


def setup_inputs():
    s = mx_kscale(DIM)
    return {"x": bf(np.random.standard_normal((B, S, DIM)) * s),
            "wq": bf(np.random.standard_normal((E, DIM)) / np.sqrt(DIM) / s[None, :]),
            "wk": bf(np.random.standard_normal((E, DIM)) / np.sqrt(DIM) / s[None, :])}


def reference(x, wq, wk):
    xq = mxq(f64(x), 2, "e5m2")
    q = (xq @ mxq(f64(wq), 1, "e5m2").T).reshape(B, S, H, D)
    k = (xq @ mxq(f64(wk), 1, "e5m2").T).reshape(B, S, H, D)
    return rope(q), rope(k)

@@ -1,0 +1,262 @@
+import math
+from contextlib import ExitStack
+
+import concourse.mybir as mybir
+from concourse.masks import make_identity
+
+B, S, DIM, H, D = 2, 256, 2048, 16, 128
+E = H * D
+ROPE_THETA = 10000.0
+FLOPS = 2 * B * S * DIM * 2 * E
+
+F32 = mybir.dt.float32
+BF16 = mybir.dt.bfloat16
+I32 = mybir.dt.int32
+U32 = mybir.dt.uint32
+U8 = mybir.dt.uint8
+E5M2X4 = mybir.dt.float8_e5m2_x4
+ALU = mybir.AluOpType
+ACT = mybir.ActivationFunctionType
+
+P = 128
+PASSES = DIM // 512
+HALF = D // 2
+N_TILE = 512
+HEADS = N_TILE // D
+CHUNKS = 2 * E // N_TILE
+STEPS = 2 * CHUNKS
+TOKEN_TILES = B * S // P
+RAW_BUFS = 6
+OUT_BUFS = 4
+PROD_BUFS = 3
+SORTED_UNITS = [(0, 1), (1, 1)]
+FIRST_SORTED_STEP = 2
+
+
+def tile_multiheadattention_pa_kernel(tc, x, wq, wk, out_0, out_1):
+    nc = tc.nc
+    x_rows = x.rearrange("b s k -> (b s) k")
+    out_rows = [o.rearrange("b s h d -> (b s) (h d)") for o in (out_0, out_1)]
+
+    with ExitStack() as ctx:
+        sb = ctx.enter_context(tc.tile_pool(name="sb", bufs=1))
+        ps = ctx.enter_context(tc.psum_pool(name="ps", bufs=1))
+        ctx.enter_context(tc.manual_schedule())
+
+        def ring(pool, label, count, shape, dtype, **kw):
+            return [pool.tile(shape, dtype, name="%s%d" % (label, i), **kw) for i in range(count)]
+
+        x_raw = ring(sb, "x_raw", TOKEN_TILES, [P, DIM], BF16)
+        x_grouped = ring(sb, "x_grouped", TOKEN_TILES, [P, DIM], BF16, align_bytes=64)
+        x_codes = ring(sb, "x_codes", TOKEN_TILES, [P, PASSES * P], U32, align_bytes=64)
+        x_scales = ring(sb, "x_scales", TOKEN_TILES, [P, PASSES * P], U8, align_bytes=64)
+        w_raw = ring(sb, "w_raw", RAW_BUFS, [P, 2, DIM], BF16)
+        w_sorted = ring(sb, "w_sorted", 2, [P, 2, PASSES, 2, P], F32)
+        w_grouped = ring(sb, "w_grouped", 2, [P, 2 * DIM], BF16, align_bytes=64)
+        w_codes = ring(sb, "w_codes", 2, [P, PASSES, N_TILE], U32, align_bytes=64)
+        w_scales = ring(sb, "w_scales", 2, [P, PASSES, N_TILE], U8, align_bytes=64)
+        prod_lo = ring(sb, "prod_lo", PROD_BUFS, [P, HEADS, 2, HALF], F32)
+        prod_hi = ring(sb, "prod_hi", PROD_BUFS, [P, HEADS, 2, HALF], F32)
+        rotated = ring(sb, "rotated", OUT_BUFS, [P, 2, N_TILE], F32)
+        turned = ring(ps, "turned", 4, [P, 2, 2, P], F32)
+        acc = ring(ps, "acc", 4, [P, N_TILE], F32)
+        ident = sb.tile([P, P], F32)
+        pos = sb.tile([P, 2, 1], I32)
+        turns = sb.tile([P, 2, 2, HALF], F32)
+        whole = sb.tile([P, 2, 2, HALF], I32)
+        frac = sb.tile([P, 2, 2, HALF], F32)
+        folded = sb.tile([P, 2, 2, HALF], F32)
+        table = sb.tile([P, 2, 3, HALF], F32)
+
+        def weight_rows(step):
+            w = (wq, wk)[step // (STEPS // 2)]
+            first = (step % (STEPS // 2)) * 2 * P
+            return w[first : first + 2 * P, :]
+
+        def load_weights(step):
+            nc.sync.dma_start(
+                out=w_raw[step % RAW_BUFS][:], in_=weight_rows(step).rearrange("(t p) k -> p t k", p=P)
+            )
+
+        for half in range(2):
+            cols = slice(half * DIM // 2, (half + 1) * DIM // 2)
+            nc.sync.dma_start(out=x_raw[0][:, cols], in_=x_rows[0:P, cols])
+        for step in range(2):
+            for t in range(2):
+                nc.sync.dma_start(out=w_raw[step][:, t, :], in_=weight_rows(step)[t * P : (t + 1) * P, :])
+        for tt in range(1, TOKEN_TILES):
+            nc.sync.dma_start(out=x_raw[tt][:], in_=x_rows[tt * P : (tt + 1) * P, :])
+        for step in range(2, RAW_BUFS):
+            load_weights(step)
+
+        nc.gpsimd.iota(pos[:], pattern=[[P, 2], [0, 1]], base=0, channel_multiplier=1)
+        make_identity(nc, ident[:])
+        angle = turns[:, :, 1, :]
+        for j in range(8):
+            nc.vector.tensor_scalar(
+                out=angle[:, :, j : j + 1], in0=pos[:],
+                scalar1=ROPE_THETA ** (-j / HALF) / (2 * math.pi), scalar2=None, op0=ALU.mult,
+            )
+        for j in range(8, HALF, 8):
+            nc.vector.tensor_scalar(
+                out=angle[:, :, j : j + 8], in0=angle[:, :, 0:8],
+                scalar1=ROPE_THETA ** (-j / HALF), scalar2=None, op0=ALU.mult,
+            )
+        nc.vector.tensor_scalar(out=turns[:, :, 0, :], in0=angle, scalar1=0.25, scalar2=None, op0=ALU.add)
+        nc.vector.tensor_copy(out=whole[:], in_=turns[:])
+        nc.vector.tensor_tensor(out=frac[:], in0=turns[:], in1=whole[:], op=ALU.subtract)
+        flat = "p a b j -> p (a b j)"
+        nc.vector.scalar_tensor_tensor(
+            out=folded[:].rearrange(flat), in0=frac[:].rearrange(flat), scalar=0.5,
+            in1=frac[:].rearrange(flat), op0=ALU.is_gt, op1=ALU.subtract,
+        )
+        nc.scalar.activation(out=table[:, :, 1:3, :], in_=folded[:], func=ACT.Sin, scale=-2 * math.pi)
+        nc.scalar.activation(out=table[:, :, 0, :], in_=folded[:, :, 1, :], func=ACT.Sin, scale=2 * math.pi)
+
+        bank_count = []
+
+        def turn(sources, dest):
+            bank = turned[len(bank_count) % len(turned)]
+            bank_count.append(1)
+            for g in range(2):
+                for u in range(2):
+                    nc.tensor.transpose(bank[:, g, u, :], sources[g][u], ident[:])
+            nc.scalar.copy(out=dest, in_=bank[:].rearrange("p g u r -> p g r u"))
+
+        def stepped(words, pair):
+            return [[words[:, 256 * g + u : 256 * (g + 1) : 2] for u in range(2)] for g in (2 * pair, 2 * pair + 1)]
+
+        def turn_x(tt):
+            words = x_raw[tt][:].bitcast(F32)
+            dest = x_grouped[tt][:].bitcast(F32).rearrange("p (g r u) -> p g r u", g=PASSES, u=2)
+            for pair in range(2):
+                turn(stepped(words, pair), dest[:, 2 * pair : 2 * pair + 2])
+
+        def quantize_x(tt):
+            nc.vector.quantize_mx(
+                out=x_codes[tt][:].bitcast(E5M2X4), scales=x_scales[tt][:], in_=x_grouped[tt][:]
+            )
+
+        def is_sorted(step, unit):
+            return step >= FIRST_SORTED_STEP and unit in SORTED_UNITS
+
+        def sort_w(step):
+            words = w_raw[step % RAW_BUFS][:].bitcast(F32)
+            for t, pair in SORTED_UNITS:
+                src = words[:, t, 512 * pair : 512 * (pair + 1)].rearrange("p (g m u) -> p g u m", g=2, u=2)
+                nc.scalar.copy(out=w_sorted[step % 2][:, t, 2 * pair : 2 * pair + 2], in_=src)
+
+        def turn_w(step, units):
+            words = w_raw[step % RAW_BUFS][:].bitcast(F32)
+            dest = w_grouped[step % 2][:].bitcast(F32).rearrange("p (g t r u) -> p g t r u", g=PASSES, t=2, u=2)
+            for t, pair in units:
+                if is_sorted(step, (t, pair)):
+                    sources = [[w_sorted[step % 2][:, t, g, u, :] for u in range(2)] for g in (2 * pair, 2 * pair + 1)]
+                else:
+                    sources = stepped(words[:, t, :], pair)
+                turn(sources, dest[:, 2 * pair : 2 * pair + 2, t])
+
+        def quantize_w(step):
+            chunk, half = divmod(step, 2)
+            cols = slice(half * 2 * P, (half + 1) * 2 * P)
+            for g in range(PASSES):
+                nc.vector.quantize_mx(
+                    out=w_codes[chunk % 2][:, g, cols].bitcast(E5M2X4),
+                    scales=w_scales[chunk % 2][:, g, cols],
+                    in_=w_grouped[step % 2][:, g * 8 * P : (g + 1) * 8 * P],
+                )
+
+        def multiply(group):
+            chunk, tt = divmod(group, TOKEN_TILES)
+            for g in range(PASSES):
+                cols = slice(g * P, (g + 1) * P)
+                nc.tensor.matmul_mx(
+                    out=acc[group % len(acc)][:],
+                    lhsT=x_codes[tt][:, cols].bitcast(E5M2X4),
+                    lhsT_scale=x_scales[tt][:, cols],
+                    rhs=w_codes[chunk % 2][:, g, :].bitcast(E5M2X4),
+                    rhs_scale=w_scales[chunk % 2][:, g, :],
+                    start=(g == 0),
+                    stop=(g == PASSES - 1),
+                )
+
+        def rotate(group):
+            chunk, tt = divmod(group, TOKEN_TILES)
+            shape = [P, HEADS, 2, HALF]
+            t = acc[group % len(acc)][:].rearrange("p (h a j) -> p h a j", h=HEADS, a=2)
+            rows = table[:, tt % 2 : tt % 2 + 1]
+            lo, hi = prod_lo[group % PROD_BUFS], prod_hi[group % PROD_BUFS]
+            nc.vector.tensor_tensor(
+                out=lo[:], in0=t[:, :, 0:1, :].to_broadcast(shape),
+                in1=rows[:, :, 1:3, :].to_broadcast(shape), op=ALU.mult,
+            )
+            nc.vector.tensor_tensor(
+                out=hi[:], in0=t[:, :, 1:2, :].to_broadcast(shape),
+                in1=rows[:, :, 0:2, :].to_broadcast(shape), op=ALU.mult,
+            )
+            last = group == CHUNKS * TOKEN_TILES - 1
+            adder = nc.vector if last else nc.gpsimd
+            result = rotated[(group // 2) % OUT_BUFS]
+            flat_h = "p h a j -> p (h a j)"
+            adder.tensor_tensor(
+                out=result[:, tt % 2, :], in0=lo[:].rearrange(flat_h), in1=hi[:].rearrange(flat_h), op=ALU.add
+            )
+            dest = out_rows[chunk // (CHUNKS // 2)]
+            first_col = (chunk % (CHUNKS // 2)) * N_TILE
+            cols = slice(first_col, first_col + N_TILE)
+            if group >= CHUNKS * TOKEN_TILES - 2:
+                nc.sync.dma_start(out=dest[tt * P : (tt + 1) * P, cols], in_=result[:, tt % 2, :])
+            elif tt % 2 == 1:
+                nc.sync.dma_start(
+                    out=dest[(tt - 1) * P : (tt + 1) * P, cols].rearrange("(t p) c -> p t c", p=P), in_=result[:]
+                )
+
+        by_tile = [(0, 0), (0, 1), (1, 0), (1, 1)]
+        by_pair = [(0, 0), (1, 0), (0, 1), (1, 1)]
+
+        def after_turn(step):
+            if step + RAW_BUFS < STEPS:
+                load_weights(step + RAW_BUFS)
+
+        def sort_next(step):
+            if FIRST_SORTED_STEP <= step + 1 < STEPS:
+                sort_w(step + 1)
+
+        turn_x(0)
+        quantize_x(0)
+        for step in range(2):
+            turn_w(step, by_tile)
+            quantize_w(step)
+        turn_x(1)
+        quantize_x(1)
+        multiply(0)
+        turn_x(2)
+        turn_x(3)
+        rotate(0)
+        quantize_x(2)
+        quantize_x(3)
+        after_turn(0)
+        after_turn(1)
+        sort_next(1)
+        multiply(1)
+        for step in range(2, 4):
+            turn_w(step, by_pair)
+            after_turn(step)
+            rotate(step - 1)
+            quantize_w(step)
+            sort_next(step)
+            multiply(step)
+        for step in range(4, STEPS):
+            group = 2 * step - 4
+            turn_w(step, by_pair)
+            after_turn(step)
+            rotate(group - 1)
+            quantize_w(step)
+            sort_next(step)
+            multiply(group)
+            rotate(group)
+            multiply(group + 1)
+        for group in range(2 * STEPS - 4, CHUNKS * TOKEN_TILES):
+            multiply(group)
+            rotate(group - 1)
+        rotate(CHUNKS * TOKEN_TILES - 1)

@@ -19,82 +19,99 @@ ALU = mybir.AluOpType
 ACT = mybir.ActivationFunctionType
 
 P = 128
-PASSES = DIM // 512
+PACK = 4
+PASSES = DIM // (P * PACK)
+PASS_WORDS = P * PACK // 2
 HALF = D // 2
 N_TILE = 512
 HEADS = N_TILE // D
 CHUNKS = 2 * E // N_TILE
-STEPS = 2 * CHUNKS
+ROW_TILES = N_TILE // P
 TOKEN_TILES = B * S // P
+POSITION_TILES = S // P
+GROUPS = CHUNKS * TOKEN_TILES
+LOADS = 2 * CHUNKS
+RUN = 4
+
 RAW_BUFS = 6
 OUT_BUFS = 4
-PROD_BUFS = 3
-SORTED_UNITS = [(0, 1), (1, 1)]
-FIRST_SORTED_STEP = 2
+PRODUCT_BUFS = 3
+SORT_BUFS = 6
+
+SORTED_AFTER_TWO = 3
+SORTED_AFTER_ONE = 2
+SCALAR_ONLY_RUNS = 2
+VECTOR_SUMS = 2
 
 
 def tile_multiheadattention_pa_kernel(tc, x, wq, wk, out_0, out_1):
     nc = tc.nc
     x_rows = x.rearrange("b s k -> (b s) k")
-    out_rows = [o.rearrange("b s h d -> (b s) (h d)") for o in (out_0, out_1)]
+    out_rows = [out.rearrange("b s h d -> (b s) (h d)") for out in (out_0, out_1)]
 
     with ExitStack() as ctx:
-        sb = ctx.enter_context(tc.tile_pool(name="sb", bufs=1))
-        ps = ctx.enter_context(tc.psum_pool(name="ps", bufs=1))
+        sbuf = ctx.enter_context(tc.tile_pool(name="sbuf", bufs=1))
+        psum = ctx.enter_context(tc.psum_pool(name="psum", bufs=1))
         ctx.enter_context(tc.manual_schedule())
 
-        def ring(pool, label, count, shape, dtype, **kw):
-            return [pool.tile(shape, dtype, name="%s%d" % (label, i), **kw) for i in range(count)]
+        def tiles(pool, label, number, shape, dtype, **options):
+            return [pool.tile(shape, dtype, name="%s%d" % (label, i), **options) for i in range(number)]
 
-        x_raw = ring(sb, "x_raw", TOKEN_TILES, [P, DIM], BF16)
-        x_grouped = ring(sb, "x_grouped", TOKEN_TILES, [P, DIM], BF16, align_bytes=64)
-        x_codes = ring(sb, "x_codes", TOKEN_TILES, [P, PASSES * P], U32, align_bytes=64)
-        x_scales = ring(sb, "x_scales", TOKEN_TILES, [P, PASSES * P], U8, align_bytes=64)
-        w_raw = ring(sb, "w_raw", RAW_BUFS, [P, 2, DIM], BF16)
-        w_sorted = ring(sb, "w_sorted", 2, [P, 2, PASSES, 2, P], F32)
-        w_grouped = ring(sb, "w_grouped", 2, [P, 2 * DIM], BF16, align_bytes=64)
-        w_codes = ring(sb, "w_codes", 2, [P, PASSES, N_TILE], U32, align_bytes=64)
-        w_scales = ring(sb, "w_scales", 2, [P, PASSES, N_TILE], U8, align_bytes=64)
-        prod_lo = ring(sb, "prod_lo", PROD_BUFS, [P, HEADS, 2, HALF], F32)
-        prod_hi = ring(sb, "prod_hi", PROD_BUFS, [P, HEADS, 2, HALF], F32)
-        rotated = ring(sb, "rotated", OUT_BUFS, [P, 2, N_TILE], F32)
-        turned = ring(ps, "turned", 4, [P, 2, 2, P], F32)
-        acc = ring(ps, "acc", 4, [P, N_TILE], F32)
-        ident = sb.tile([P, P], F32)
-        pos = sb.tile([P, 2, 1], I32)
-        turns = sb.tile([P, 2, 2, HALF], F32)
-        whole = sb.tile([P, 2, 2, HALF], I32)
-        frac = sb.tile([P, 2, 2, HALF], F32)
-        folded = sb.tile([P, 2, 2, HALF], F32)
-        table = sb.tile([P, 2, 3, HALF], F32)
+        x_raw = tiles(sbuf, "x_raw", TOKEN_TILES, [P, DIM], BF16)
+        x_turned = tiles(sbuf, "x_turned", TOKEN_TILES, [P, DIM], BF16, align_bytes=64)
+        x_codes = tiles(sbuf, "x_codes", TOKEN_TILES, [P, PASSES * P], U32, align_bytes=64)
+        x_scales = tiles(sbuf, "x_scales", TOKEN_TILES, [P, PASSES * P], U8, align_bytes=64)
+        w_raw = tiles(sbuf, "w_raw", RAW_BUFS, [P, 2, DIM], BF16)
+        w_turned = tiles(sbuf, "w_turned", 2, [P, 2 * N_TILE * PACK], BF16, align_bytes=64)
+        w_codes = tiles(sbuf, "w_codes", 2, [P, PASSES, N_TILE], U32, align_bytes=64)
+        w_scales = tiles(sbuf, "w_scales", 2, [P, PASSES, N_TILE], U8, align_bytes=64)
+        sorted_words = tiles(sbuf, "sorted_words", SORT_BUFS, [P, 2, 2, P], F32)
+        from_lower = tiles(sbuf, "from_lower", PRODUCT_BUFS, [P, HEADS, 2, HALF], F32)
+        from_upper = tiles(sbuf, "from_upper", PRODUCT_BUFS, [P, HEADS, 2, HALF], F32)
+        rotated = tiles(sbuf, "rotated", OUT_BUFS, [P, 2, N_TILE], F32)
+        turn_banks = tiles(psum, "turn_bank", RUN, [P, 2, 2, P], F32)
+        sum_banks = tiles(psum, "sum_bank", 4, [P, N_TILE], F32)
+        identity = sbuf.tile([P, P], F32)
+        position = sbuf.tile([P, POSITION_TILES, 1], I32)
+        turns = sbuf.tile([P, POSITION_TILES, 2, HALF], F32)
+        whole_turns = sbuf.tile([P, POSITION_TILES, 2, HALF], I32)
+        rest = sbuf.tile([P, POSITION_TILES, 2, HALF], F32)
+        folded = sbuf.tile([P, POSITION_TILES, 2, HALF], F32)
+        table = sbuf.tile([P, POSITION_TILES, 3, HALF], F32)
+        banks_used = []
+        sorts_done = []
 
-        def weight_rows(step):
-            w = (wq, wk)[step // (STEPS // 2)]
-            first = (step % (STEPS // 2)) * 2 * P
-            return w[first : first + 2 * P, :]
+        def weight_rows(load):
+            weights = (wq, wk)[load // CHUNKS]
+            first = (load % CHUNKS) * 2 * P
+            return weights[first : first + 2 * P, :]
 
-        def load_weights(step):
-            nc.sync.dma_start(
-                out=w_raw[step % RAW_BUFS][:], in_=weight_rows(step).rearrange("(t p) k -> p t k", p=P)
-            )
+        def load_weights(load):
+            rows = weight_rows(load).rearrange("(t p) k -> p t k", p=P)
+            nc.sync.dma_start(out=w_raw[load % RAW_BUFS][:], in_=rows)
+
+        def refill(chunk):
+            for load in (2 * chunk + RAW_BUFS, 2 * chunk + 1 + RAW_BUFS):
+                if load < LOADS:
+                    load_weights(load)
 
         for half in range(2):
-            cols = slice(half * DIM // 2, (half + 1) * DIM // 2)
-            nc.sync.dma_start(out=x_raw[0][:, cols], in_=x_rows[0:P, cols])
-        for step in range(2):
+            columns = slice(half * DIM // 2, (half + 1) * DIM // 2)
+            nc.sync.dma_start(out=x_raw[0][:, columns], in_=x_rows[0:P, columns])
+        for load in range(2):
             for t in range(2):
-                nc.sync.dma_start(out=w_raw[step][:, t, :], in_=weight_rows(step)[t * P : (t + 1) * P, :])
+                nc.sync.dma_start(out=w_raw[load][:, t, :], in_=weight_rows(load)[t * P : (t + 1) * P, :])
         for tt in range(1, TOKEN_TILES):
             nc.sync.dma_start(out=x_raw[tt][:], in_=x_rows[tt * P : (tt + 1) * P, :])
-        for step in range(2, RAW_BUFS):
-            load_weights(step)
+        for load in range(2, RAW_BUFS):
+            load_weights(load)
 
-        nc.gpsimd.iota(pos[:], pattern=[[P, 2], [0, 1]], base=0, channel_multiplier=1)
-        make_identity(nc, ident[:])
+        nc.gpsimd.iota(position[:], pattern=[[P, POSITION_TILES], [0, 1]], base=0, channel_multiplier=1)
+        make_identity(nc, identity[:])
         angle = turns[:, :, 1, :]
         for j in range(8):
             nc.vector.tensor_scalar(
-                out=angle[:, :, j : j + 1], in0=pos[:],
+                out=angle[:, :, j : j + 1], in0=position[:],
                 scalar1=ROPE_THETA ** (-j / HALF) / (2 * math.pi), scalar2=None, op0=ALU.mult,
             )
         for j in range(8, HALF, 8):
@@ -103,160 +120,173 @@ def tile_multiheadattention_pa_kernel(tc, x, wq, wk, out_0, out_1):
                 scalar1=ROPE_THETA ** (-j / HALF), scalar2=None, op0=ALU.mult,
             )
         nc.vector.tensor_scalar(out=turns[:, :, 0, :], in0=angle, scalar1=0.25, scalar2=None, op0=ALU.add)
-        nc.vector.tensor_copy(out=whole[:], in_=turns[:])
-        nc.vector.tensor_tensor(out=frac[:], in0=turns[:], in1=whole[:], op=ALU.subtract)
-        flat = "p a b j -> p (a b j)"
+        nc.vector.tensor_copy(out=whole_turns[:], in_=turns[:])
+        nc.vector.tensor_tensor(out=rest[:], in0=turns[:], in1=whole_turns[:], op=ALU.subtract)
+        flat_table = "p i c j -> p (i c j)"
         nc.vector.scalar_tensor_tensor(
-            out=folded[:].rearrange(flat), in0=frac[:].rearrange(flat), scalar=0.5,
-            in1=frac[:].rearrange(flat), op0=ALU.is_gt, op1=ALU.subtract,
+            out=folded[:].rearrange(flat_table), in0=rest[:].rearrange(flat_table), scalar=0.5,
+            in1=rest[:].rearrange(flat_table), op0=ALU.is_gt, op1=ALU.subtract,
         )
         nc.scalar.activation(out=table[:, :, 1:3, :], in_=folded[:], func=ACT.Sin, scale=-2 * math.pi)
         nc.scalar.activation(out=table[:, :, 0, :], in_=folded[:, :, 1, :], func=ACT.Sin, scale=2 * math.pi)
 
-        bank_count = []
+        def x_piece(tt, pair):
+            words = x_raw[tt][:].bitcast(F32)[:, 2 * pair * PASS_WORDS : 2 * (pair + 1) * PASS_WORDS]
+            target = x_turned[tt][:].bitcast(F32).rearrange("p (g r u) -> p g r u", g=PASSES, u=2)
+            return words, target[:, 2 * pair : 2 * pair + 2]
 
-        def turn(sources, dest):
-            bank = turned[len(bank_count) % len(turned)]
-            bank_count.append(1)
-            for g in range(2):
-                for u in range(2):
-                    nc.tensor.transpose(bank[:, g, u, :], sources[g][u], ident[:])
-            nc.scalar.copy(out=dest, in_=bank[:].rearrange("p g u r -> p g r u"))
+        def w_piece(chunk, t, pair):
+            raw = w_raw[(2 * chunk + t // 2) % RAW_BUFS][:].bitcast(F32)
+            words = raw[:, t % 2, 2 * pair * PASS_WORDS : 2 * (pair + 1) * PASS_WORDS]
+            target = w_turned[pair][:].bitcast(F32).rearrange("p (g t r u) -> p g t r u", g=2, t=ROW_TILES, u=2)
+            return words, target[:, :, t]
 
-        def stepped(words, pair):
-            return [[words[:, 256 * g + u : 256 * (g + 1) : 2] for u in range(2)] for g in (2 * pair, 2 * pair + 1)]
+        def prepare(pieces, sort):
+            ready = []
+            for i, (words, target) in enumerate(pieces):
+                view = words.rearrange("r (g m u) -> r g u m", g=2, u=2)
+                if i >= len(pieces) - sort:
+                    held = sorted_words[len(sorts_done) % SORT_BUFS]
+                    sorts_done.append(held)
+                    nc.scalar.copy(out=held[:], in_=view)
+                    view = held[:]
+                ready.append((view, target))
+            return ready
 
-        def turn_x(tt):
-            words = x_raw[tt][:].bitcast(F32)
-            dest = x_grouped[tt][:].bitcast(F32).rearrange("p (g r u) -> p g r u", g=PASSES, u=2)
-            for pair in range(2):
-                turn(stepped(words, pair), dest[:, 2 * pair : 2 * pair + 2])
+        def turn(ready, on_vector=()):
+            for i, (view, target) in enumerate(ready):
+                bank = turn_banks[len(banks_used) % RUN]
+                banks_used.append(bank)
+                for g in range(2):
+                    for u in range(2):
+                        nc.tensor.transpose(bank[:, g, u, :], view[:, g, u, :], identity[:])
+                source = bank[:].rearrange("p g u r -> p g r u")
+                if i in on_vector:
+                    nc.vector.tensor_copy(out=target, in_=source)
+                else:
+                    nc.scalar.copy(out=target, in_=source)
 
         def quantize_x(tt):
+            nc.vector.quantize_mx(out=x_codes[tt][:].bitcast(E5M2X4), scales=x_scales[tt][:], in_=x_turned[tt][:])
+
+        def quantize_pair(chunk, pair):
+            passes = slice(2 * pair, 2 * pair + 2)
+            flat_passes = "p g n -> p (g n)"
             nc.vector.quantize_mx(
-                out=x_codes[tt][:].bitcast(E5M2X4), scales=x_scales[tt][:], in_=x_grouped[tt][:]
+                out=w_codes[chunk % 2][:, passes, :].rearrange(flat_passes).bitcast(E5M2X4),
+                scales=w_scales[chunk % 2][:, passes, :].rearrange(flat_passes),
+                in_=w_turned[pair][:],
             )
 
-        def is_sorted(step, unit):
-            return step >= FIRST_SORTED_STEP and unit in SORTED_UNITS
-
-        def sort_w(step):
-            words = w_raw[step % RAW_BUFS][:].bitcast(F32)
-            for t, pair in SORTED_UNITS:
-                src = words[:, t, 512 * pair : 512 * (pair + 1)].rearrange("p (g m u) -> p g u m", g=2, u=2)
-                nc.scalar.copy(out=w_sorted[step % 2][:, t, 2 * pair : 2 * pair + 2], in_=src)
-
-        def turn_w(step, units):
-            words = w_raw[step % RAW_BUFS][:].bitcast(F32)
-            dest = w_grouped[step % 2][:].bitcast(F32).rearrange("p (g t r u) -> p g t r u", g=PASSES, t=2, u=2)
-            for t, pair in units:
-                if is_sorted(step, (t, pair)):
-                    sources = [[w_sorted[step % 2][:, t, g, u, :] for u in range(2)] for g in (2 * pair, 2 * pair + 1)]
-                else:
-                    sources = stepped(words[:, t, :], pair)
-                turn(sources, dest[:, 2 * pair : 2 * pair + 2, t])
-
-        def quantize_w(step):
-            chunk, half = divmod(step, 2)
-            cols = slice(half * 2 * P, (half + 1) * 2 * P)
+        def quantize_half(chunk, half):
+            rows = slice(half * 2 * P, (half + 1) * 2 * P)
             for g in range(PASSES):
+                first = ((g % 2) * N_TILE + rows.start) * PACK
                 nc.vector.quantize_mx(
-                    out=w_codes[chunk % 2][:, g, cols].bitcast(E5M2X4),
-                    scales=w_scales[chunk % 2][:, g, cols],
-                    in_=w_grouped[step % 2][:, g * 8 * P : (g + 1) * 8 * P],
+                    out=w_codes[chunk % 2][:, g, rows].bitcast(E5M2X4),
+                    scales=w_scales[chunk % 2][:, g, rows],
+                    in_=w_turned[g // 2][:, first : first + 2 * P * PACK],
                 )
 
         def multiply(group):
             chunk, tt = divmod(group, TOKEN_TILES)
             for g in range(PASSES):
-                cols = slice(g * P, (g + 1) * P)
+                tokens = slice(g * P, (g + 1) * P)
                 nc.tensor.matmul_mx(
-                    out=acc[group % len(acc)][:],
-                    lhsT=x_codes[tt][:, cols].bitcast(E5M2X4),
-                    lhsT_scale=x_scales[tt][:, cols],
+                    out=sum_banks[group % len(sum_banks)][:],
+                    lhsT=x_codes[tt][:, tokens].bitcast(E5M2X4),
+                    lhsT_scale=x_scales[tt][:, tokens],
                     rhs=w_codes[chunk % 2][:, g, :].bitcast(E5M2X4),
                     rhs_scale=w_scales[chunk % 2][:, g, :],
                     start=(g == 0),
                     stop=(g == PASSES - 1),
                 )
 
-        def rotate(group):
+        def add_and_store(group, engine):
             chunk, tt = divmod(group, TOKEN_TILES)
-            shape = [P, HEADS, 2, HALF]
-            t = acc[group % len(acc)][:].rearrange("p (h a j) -> p h a j", h=HEADS, a=2)
-            rows = table[:, tt % 2 : tt % 2 + 1]
-            lo, hi = prod_lo[group % PROD_BUFS], prod_hi[group % PROD_BUFS]
-            nc.vector.tensor_tensor(
-                out=lo[:], in0=t[:, :, 0:1, :].to_broadcast(shape),
-                in1=rows[:, :, 1:3, :].to_broadcast(shape), op=ALU.mult,
-            )
-            nc.vector.tensor_tensor(
-                out=hi[:], in0=t[:, :, 1:2, :].to_broadcast(shape),
-                in1=rows[:, :, 0:2, :].to_broadcast(shape), op=ALU.mult,
-            )
-            last = group == CHUNKS * TOKEN_TILES - 1
-            adder = nc.vector if last else nc.gpsimd
             result = rotated[(group // 2) % OUT_BUFS]
-            flat_h = "p h a j -> p (h a j)"
-            adder.tensor_tensor(
-                out=result[:, tt % 2, :], in0=lo[:].rearrange(flat_h), in1=hi[:].rearrange(flat_h), op=ALU.add
+            flat_heads = "p h c j -> p (h c j)"
+            engine.tensor_tensor(
+                out=result[:, tt % 2, :],
+                in0=from_lower[group % PRODUCT_BUFS][:].rearrange(flat_heads),
+                in1=from_upper[group % PRODUCT_BUFS][:].rearrange(flat_heads),
+                op=ALU.add,
             )
-            dest = out_rows[chunk // (CHUNKS // 2)]
-            first_col = (chunk % (CHUNKS // 2)) * N_TILE
-            cols = slice(first_col, first_col + N_TILE)
-            if group >= CHUNKS * TOKEN_TILES - 2:
-                nc.sync.dma_start(out=dest[tt * P : (tt + 1) * P, cols], in_=result[:, tt % 2, :])
+            out = out_rows[chunk // (CHUNKS // 2)]
+            first = (chunk % (CHUNKS // 2)) * N_TILE
+            features = slice(first, first + N_TILE)
+            if chunk == CHUNKS - 1:
+                nc.sync.dma_start(out=out[tt * P : (tt + 1) * P, features], in_=result[:, tt % 2, :])
             elif tt % 2 == 1:
-                nc.sync.dma_start(
-                    out=dest[(tt - 1) * P : (tt + 1) * P, cols].rearrange("(t p) c -> p t c", p=P), in_=result[:]
-                )
+                rows = out[(tt - 1) * P : (tt + 1) * P, features]
+                nc.sync.dma_start(out=rows.rearrange("(t p) n -> p t n", p=P), in_=result[:])
 
-        by_tile = [(0, 0), (0, 1), (1, 0), (1, 1)]
-        by_pair = [(0, 0), (1, 0), (0, 1), (1, 1)]
+        def rotate(group):
+            shape = [P, HEADS, 2, HALF]
+            sums = sum_banks[group % len(sum_banks)][:].rearrange("p (h c j) -> p h c j", h=HEADS, c=2)
+            i = group % POSITION_TILES
+            nc.vector.tensor_tensor(
+                out=from_lower[group % PRODUCT_BUFS][:], in0=sums[:, :, 0:1, :].to_broadcast(shape),
+                in1=table[:, i : i + 1, 1:3, :].to_broadcast(shape), op=ALU.mult,
+            )
+            nc.vector.tensor_tensor(
+                out=from_upper[group % PRODUCT_BUFS][:], in0=sums[:, :, 1:2, :].to_broadcast(shape),
+                in1=table[:, i : i + 1, 0:2, :].to_broadcast(shape), op=ALU.mult,
+            )
+            if group < GROUPS - VECTOR_SUMS:
+                add_and_store(group, nc.gpsimd)
 
-        def after_turn(step):
-            if step + RAW_BUFS < STEPS:
-                load_weights(step + RAW_BUFS)
+        def half_by_rows(chunk, half):
+            return [w_piece(chunk, t, pair) for t in (2 * half, 2 * half + 1) for pair in range(2)]
 
-        def sort_next(step):
-            if FIRST_SORTED_STEP <= step + 1 < STEPS:
-                sort_w(step + 1)
+        def pair_by_passes(chunk, pair):
+            return [w_piece(chunk, t, pair) for t in range(ROW_TILES)]
 
-        turn_x(0)
+        turn(prepare([x_piece(0, pair) for pair in range(2)], 0))
         quantize_x(0)
-        for step in range(2):
-            turn_w(step, by_tile)
-            quantize_w(step)
-        turn_x(1)
+        for half in range(2):
+            turn(prepare(half_by_rows(0, half), 0))
+            quantize_half(0, half)
+        turn(prepare([x_piece(1, pair) for pair in range(2)], 0))
+        ready = prepare([x_piece(tt, pair) for tt in (2, 3) for pair in range(2)], SORTED_AFTER_TWO)
         quantize_x(1)
         multiply(0)
-        turn_x(2)
-        turn_x(3)
-        rotate(0)
+        turn(ready, on_vector=(1, 3))
+        refill(0)
+        ready = prepare(half_by_rows(1, 0), SORTED_AFTER_ONE)
         quantize_x(2)
+        rotate(0)
         quantize_x(3)
-        after_turn(0)
-        after_turn(1)
-        sort_next(1)
         multiply(1)
-        for step in range(2, 4):
-            turn_w(step, by_pair)
-            after_turn(step)
-            rotate(step - 1)
-            quantize_w(step)
-            sort_next(step)
-            multiply(step)
-        for step in range(4, STEPS):
-            group = 2 * step - 4
-            turn_w(step, by_pair)
-            after_turn(step)
+        rotate(1)
+        turn(ready)
+        ready = prepare(half_by_rows(1, 1), SORTED_AFTER_ONE)
+        quantize_half(1, 0)
+        multiply(2)
+        rotate(2)
+        turn(ready)
+        refill(1)
+        ready = prepare(pair_by_passes(2, 0), SORTED_AFTER_ONE)
+        quantize_half(1, 1)
+        multiply(3)
+
+        steps = [(chunk, pair) for chunk in range(2, CHUNKS) for pair in range(2)]
+        for i, (chunk, pair) in enumerate(steps):
+            group = (chunk - 1) * TOKEN_TILES + 2 * pair
             rotate(group - 1)
-            quantize_w(step)
-            sort_next(step)
+            turn(ready, on_vector=(0,) if i < len(steps) - SCALAR_ONLY_RUNS else ())
+            if pair == 1:
+                refill(chunk)
+            if i + 1 < len(steps):
+                ready = prepare(pair_by_passes(*steps[i + 1]), SORTED_AFTER_TWO)
             multiply(group)
             rotate(group)
+            quantize_pair(chunk, pair)
             multiply(group + 1)
-        for group in range(2 * STEPS - 4, CHUNKS * TOKEN_TILES):
+
+        for group in range(GROUPS - TOKEN_TILES, GROUPS):
             multiply(group)
             rotate(group - 1)
-        rotate(CHUNKS * TOKEN_TILES - 1)
+        rotate(GROUPS - 1)
+        for group in range(GROUPS - VECTOR_SUMS, GROUPS):
+            add_and_store(group, nc.vector)

import math
from contextlib import ExitStack

import concourse.mybir as mybir
from concourse.masks import make_identity

B, S, DIM, H, D = 2, 256, 2048, 16, 128
E = H * D
ROPE_THETA = 10000.0
FLOPS = 2 * B * S * DIM * 2 * E

F32 = mybir.dt.float32
BF16 = mybir.dt.bfloat16
I32 = mybir.dt.int32
U32 = mybir.dt.uint32
U8 = mybir.dt.uint8
E5M2X4 = mybir.dt.float8_e5m2_x4
ALU = mybir.AluOpType
ACT = mybir.ActivationFunctionType

P = 128
PACK = 4
PASSES = DIM // (P * PACK)
PASS_WORDS = P * PACK // 2
HALF = D // 2
N_TILE = 512
HEADS = N_TILE // D
CHUNKS = 2 * E // N_TILE
ROW_TILES = N_TILE // P
TOKEN_TILES = B * S // P
POSITION_TILES = S // P
GROUPS = CHUNKS * TOKEN_TILES
LOADS = 2 * CHUNKS
RUN = 4

RAW_BUFS = 6
OUT_BUFS = 4
PRODUCT_BUFS = 3
SORT_BUFS = 6

SORTED_AFTER_TWO = 3
SORTED_AFTER_ONE = 2
SCALAR_ONLY_RUNS = 2
VECTOR_SUMS = 2


def tile_multiheadattention_pa_kernel(tc, x, wq, wk, out_0, out_1):
    nc = tc.nc
    x_rows = x.rearrange("b s k -> (b s) k")
    out_rows = [out.rearrange("b s h d -> (b s) (h d)") for out in (out_0, out_1)]

    with ExitStack() as ctx:
        sbuf = ctx.enter_context(tc.tile_pool(name="sbuf", bufs=1))
        psum = ctx.enter_context(tc.psum_pool(name="psum", bufs=1))
        ctx.enter_context(tc.manual_schedule())

        def tiles(pool, label, number, shape, dtype, **options):
            return [pool.tile(shape, dtype, name="%s%d" % (label, i), **options) for i in range(number)]

        x_raw = tiles(sbuf, "x_raw", TOKEN_TILES, [P, DIM], BF16)
        x_turned = tiles(sbuf, "x_turned", TOKEN_TILES, [P, DIM], BF16, align_bytes=64)
        x_codes = tiles(sbuf, "x_codes", TOKEN_TILES, [P, PASSES * P], U32, align_bytes=64)
        x_scales = tiles(sbuf, "x_scales", TOKEN_TILES, [P, PASSES * P], U8, align_bytes=64)
        w_raw = tiles(sbuf, "w_raw", RAW_BUFS, [P, 2, DIM], BF16)
        w_turned = tiles(sbuf, "w_turned", 2, [P, 2 * N_TILE * PACK], BF16, align_bytes=64)
        w_codes = tiles(sbuf, "w_codes", 2, [P, PASSES, N_TILE], U32, align_bytes=64)
        w_scales = tiles(sbuf, "w_scales", 2, [P, PASSES, N_TILE], U8, align_bytes=64)
        sorted_words = tiles(sbuf, "sorted_words", SORT_BUFS, [P, 2, 2, P], F32)
        from_lower = tiles(sbuf, "from_lower", PRODUCT_BUFS, [P, HEADS, 2, HALF], F32)
        from_upper = tiles(sbuf, "from_upper", PRODUCT_BUFS, [P, HEADS, 2, HALF], F32)
        rotated = tiles(sbuf, "rotated", OUT_BUFS, [P, 2, N_TILE], F32)
        turn_banks = tiles(psum, "turn_bank", RUN, [P, 2, 2, P], F32)
        sum_banks = tiles(psum, "sum_bank", 4, [P, N_TILE], F32)
        identity = sbuf.tile([P, P], F32)
        position = sbuf.tile([P, POSITION_TILES, 1], I32)
        turns = sbuf.tile([P, POSITION_TILES, 2, HALF], F32)
        whole_turns = sbuf.tile([P, POSITION_TILES, 2, HALF], I32)
        rest = sbuf.tile([P, POSITION_TILES, 2, HALF], F32)
        folded = sbuf.tile([P, POSITION_TILES, 2, HALF], F32)
        table = sbuf.tile([P, POSITION_TILES, 3, HALF], F32)
        banks_used = []
        sorts_done = []

        def weight_rows(load):
            weights = (wq, wk)[load // CHUNKS]
            first = (load % CHUNKS) * 2 * P
            return weights[first : first + 2 * P, :]

        def load_weights(load):
            rows = weight_rows(load).rearrange("(t p) k -> p t k", p=P)
            nc.sync.dma_start(out=w_raw[load % RAW_BUFS][:], in_=rows)

        def refill(chunk):
            for load in (2 * chunk + RAW_BUFS, 2 * chunk + 1 + RAW_BUFS):
                if load < LOADS:
                    load_weights(load)

        for half in range(2):
            columns = slice(half * DIM // 2, (half + 1) * DIM // 2)
            nc.sync.dma_start(out=x_raw[0][:, columns], in_=x_rows[0:P, columns])
        for load in range(2):
            for t in range(2):
                nc.sync.dma_start(out=w_raw[load][:, t, :], in_=weight_rows(load)[t * P : (t + 1) * P, :])
        for tt in range(1, TOKEN_TILES):
            nc.sync.dma_start(out=x_raw[tt][:], in_=x_rows[tt * P : (tt + 1) * P, :])
        for load in range(2, RAW_BUFS):
            load_weights(load)

        nc.gpsimd.iota(position[:], pattern=[[P, POSITION_TILES], [0, 1]], base=0, channel_multiplier=1)
        make_identity(nc, identity[:])
        angle = turns[:, :, 1, :]
        for j in range(8):
            nc.vector.tensor_scalar(
                out=angle[:, :, j : j + 1], in0=position[:],
                scalar1=ROPE_THETA ** (-j / HALF) / (2 * math.pi), scalar2=None, op0=ALU.mult,
            )
        for j in range(8, HALF, 8):
            nc.vector.tensor_scalar(
                out=angle[:, :, j : j + 8], in0=angle[:, :, 0:8],
                scalar1=ROPE_THETA ** (-j / HALF), scalar2=None, op0=ALU.mult,
            )
        nc.vector.tensor_scalar(out=turns[:, :, 0, :], in0=angle, scalar1=0.25, scalar2=None, op0=ALU.add)
        nc.vector.tensor_copy(out=whole_turns[:], in_=turns[:])
        nc.vector.tensor_tensor(out=rest[:], in0=turns[:], in1=whole_turns[:], op=ALU.subtract)
        flat_table = "p i c j -> p (i c j)"
        nc.vector.scalar_tensor_tensor(
            out=folded[:].rearrange(flat_table), in0=rest[:].rearrange(flat_table), scalar=0.5,
            in1=rest[:].rearrange(flat_table), op0=ALU.is_gt, op1=ALU.subtract,
        )
        nc.scalar.activation(out=table[:, :, 1:3, :], in_=folded[:], func=ACT.Sin, scale=-2 * math.pi)
        nc.scalar.activation(out=table[:, :, 0, :], in_=folded[:, :, 1, :], func=ACT.Sin, scale=2 * math.pi)

        def x_piece(tt, pair):
            words = x_raw[tt][:].bitcast(F32)[:, 2 * pair * PASS_WORDS : 2 * (pair + 1) * PASS_WORDS]
            target = x_turned[tt][:].bitcast(F32).rearrange("p (g r u) -> p g r u", g=PASSES, u=2)
            return words, target[:, 2 * pair : 2 * pair + 2]

        def w_piece(chunk, t, pair):
            raw = w_raw[(2 * chunk + t // 2) % RAW_BUFS][:].bitcast(F32)
            words = raw[:, t % 2, 2 * pair * PASS_WORDS : 2 * (pair + 1) * PASS_WORDS]
            target = w_turned[pair][:].bitcast(F32).rearrange("p (g t r u) -> p g t r u", g=2, t=ROW_TILES, u=2)
            return words, target[:, :, t]

        def prepare(pieces, sort):
            ready = []
            for i, (words, target) in enumerate(pieces):
                view = words.rearrange("r (g m u) -> r g u m", g=2, u=2)
                if i >= len(pieces) - sort:
                    held = sorted_words[len(sorts_done) % SORT_BUFS]
                    sorts_done.append(held)
                    nc.scalar.copy(out=held[:], in_=view)
                    view = held[:]
                ready.append((view, target))
            return ready

        def turn(ready, on_vector=()):
            for i, (view, target) in enumerate(ready):
                bank = turn_banks[len(banks_used) % RUN]
                banks_used.append(bank)
                for g in range(2):
                    for u in range(2):
                        nc.tensor.transpose(bank[:, g, u, :], view[:, g, u, :], identity[:])
                source = bank[:].rearrange("p g u r -> p g r u")
                if i in on_vector:
                    nc.vector.tensor_copy(out=target, in_=source)
                else:
                    nc.scalar.copy(out=target, in_=source)

        def quantize_x(tt):
            nc.vector.quantize_mx(out=x_codes[tt][:].bitcast(E5M2X4), scales=x_scales[tt][:], in_=x_turned[tt][:])

        def quantize_pair(chunk, pair):
            passes = slice(2 * pair, 2 * pair + 2)
            flat_passes = "p g n -> p (g n)"
            nc.vector.quantize_mx(
                out=w_codes[chunk % 2][:, passes, :].rearrange(flat_passes).bitcast(E5M2X4),
                scales=w_scales[chunk % 2][:, passes, :].rearrange(flat_passes),
                in_=w_turned[pair][:],
            )

        def quantize_half(chunk, half):
            rows = slice(half * 2 * P, (half + 1) * 2 * P)
            for g in range(PASSES):
                first = ((g % 2) * N_TILE + rows.start) * PACK
                nc.vector.quantize_mx(
                    out=w_codes[chunk % 2][:, g, rows].bitcast(E5M2X4),
                    scales=w_scales[chunk % 2][:, g, rows],
                    in_=w_turned[g // 2][:, first : first + 2 * P * PACK],
                )

        def multiply(group):
            chunk, tt = divmod(group, TOKEN_TILES)
            for g in range(PASSES):
                tokens = slice(g * P, (g + 1) * P)
                nc.tensor.matmul_mx(
                    out=sum_banks[group % len(sum_banks)][:],
                    lhsT=x_codes[tt][:, tokens].bitcast(E5M2X4),
                    lhsT_scale=x_scales[tt][:, tokens],
                    rhs=w_codes[chunk % 2][:, g, :].bitcast(E5M2X4),
                    rhs_scale=w_scales[chunk % 2][:, g, :],
                    start=(g == 0),
                    stop=(g == PASSES - 1),
                )

        def add_and_store(group, engine):
            chunk, tt = divmod(group, TOKEN_TILES)
            result = rotated[(group // 2) % OUT_BUFS]
            flat_heads = "p h c j -> p (h c j)"
            engine.tensor_tensor(
                out=result[:, tt % 2, :],
                in0=from_lower[group % PRODUCT_BUFS][:].rearrange(flat_heads),
                in1=from_upper[group % PRODUCT_BUFS][:].rearrange(flat_heads),
                op=ALU.add,
            )
            out = out_rows[chunk // (CHUNKS // 2)]
            first = (chunk % (CHUNKS // 2)) * N_TILE
            features = slice(first, first + N_TILE)
            if chunk == CHUNKS - 1:
                nc.sync.dma_start(out=out[tt * P : (tt + 1) * P, features], in_=result[:, tt % 2, :])
            elif tt % 2 == 1:
                rows = out[(tt - 1) * P : (tt + 1) * P, features]
                nc.sync.dma_start(out=rows.rearrange("(t p) n -> p t n", p=P), in_=result[:])

        def rotate(group):
            shape = [P, HEADS, 2, HALF]
            sums = sum_banks[group % len(sum_banks)][:].rearrange("p (h c j) -> p h c j", h=HEADS, c=2)
            i = group % POSITION_TILES
            nc.vector.tensor_tensor(
                out=from_lower[group % PRODUCT_BUFS][:], in0=sums[:, :, 0:1, :].to_broadcast(shape),
                in1=table[:, i : i + 1, 1:3, :].to_broadcast(shape), op=ALU.mult,
            )
            nc.vector.tensor_tensor(
                out=from_upper[group % PRODUCT_BUFS][:], in0=sums[:, :, 1:2, :].to_broadcast(shape),
                in1=table[:, i : i + 1, 0:2, :].to_broadcast(shape), op=ALU.mult,
            )
            if group < GROUPS - VECTOR_SUMS:
                add_and_store(group, nc.gpsimd)

        def half_by_rows(chunk, half):
            return [w_piece(chunk, t, pair) for t in (2 * half, 2 * half + 1) for pair in range(2)]

        def pair_by_passes(chunk, pair):
            return [w_piece(chunk, t, pair) for t in range(ROW_TILES)]

        turn(prepare([x_piece(0, pair) for pair in range(2)], 0))
        quantize_x(0)
        for half in range(2):
            turn(prepare(half_by_rows(0, half), 0))
            quantize_half(0, half)
        turn(prepare([x_piece(1, pair) for pair in range(2)], 0))
        ready = prepare([x_piece(tt, pair) for tt in (2, 3) for pair in range(2)], SORTED_AFTER_TWO)
        quantize_x(1)
        multiply(0)
        turn(ready, on_vector=(1, 3))
        refill(0)
        ready = prepare(half_by_rows(1, 0), SORTED_AFTER_ONE)
        quantize_x(2)
        rotate(0)
        quantize_x(3)
        multiply(1)
        rotate(1)
        turn(ready)
        ready = prepare(half_by_rows(1, 1), SORTED_AFTER_ONE)
        quantize_half(1, 0)
        multiply(2)
        rotate(2)
        turn(ready)
        refill(1)
        ready = prepare(pair_by_passes(2, 0), SORTED_AFTER_ONE)
        quantize_half(1, 1)
        multiply(3)

        steps = [(chunk, pair) for chunk in range(2, CHUNKS) for pair in range(2)]
        for i, (chunk, pair) in enumerate(steps):
            group = (chunk - 1) * TOKEN_TILES + 2 * pair
            rotate(group - 1)
            turn(ready, on_vector=(0,) if i < len(steps) - SCALAR_ONLY_RUNS else ())
            if pair == 1:
                refill(chunk)
            if i + 1 < len(steps):
                ready = prepare(pair_by_passes(*steps[i + 1]), SORTED_AFTER_TWO)
            multiply(group)
            rotate(group)
            quantize_pair(chunk, pair)
            multiply(group + 1)

        for group in range(GROUPS - TOKEN_TILES, GROUPS):
            multiply(group)
            rotate(group - 1)
        rotate(GROUPS - 1)
        for group in range(GROUPS - VECTOR_SUMS, GROUPS):
            add_and_store(group, nc.vector)
